import numpy as np
import ml_dtypes


def mxq(x, axis, fmt="e4m3"):
    dtype, down = {"e4m3": (ml_dtypes.float8_e4m3fn, 7), "e5m2": (ml_dtypes.float8_e5m2, 14)}[fmt]
    v = np.moveaxis(np.asarray(x, np.float32).astype(ml_dtypes.bfloat16).astype(np.float64), axis, -1)
    blocks = v.reshape(v.shape[:-1] + (-1, 32))
    amax = np.abs(blocks).max(-1, keepdims=True)
    byte = np.maximum(np.where(amax > 0, np.frexp(amax)[1] - 1 + 127, 0) - down, 1)
    scale = np.exp2(byte - 127.0)
    codes = (blocks / scale).astype(np.float32).astype(dtype).astype(np.float64)
    return np.moveaxis((codes * scale).reshape(v.shape), -1, axis)


WIDE = False


def mx_kscale(k):
    if not WIDE:
        return np.ones(k)
    levels = np.array([10, -10, 5, -5, 0])
    if k % 512:
        return np.exp2(np.random.permutation(np.resize(levels, k // 32))).repeat(32)
    a = np.empty((k // 512, 16))
    for p in range(k // 512):
        a[p, :8] = np.random.permutation(np.resize(levels, 8))
        for g in range(8):
            far = levels[np.abs(levels - a[p, g]) >= 10]
            a[p, g + 8] = far[np.random.randint(len(far))]
    return np.exp2(a.ravel()).repeat(32)


BF16 = ml_dtypes.bfloat16


def bf(x):
    return np.asarray(x, np.float32).astype(BF16)


def f64(x):
    return np.asarray(x).astype(np.float64)


B, D, HID, G0, RIN, NR = 256, 1024, 2048, 512, 256, 5
EPS = 1e-05
W2S = 0.02


def silu(v):
    return v / (1.0 + np.exp(-v))


def setup_inputs():
    s, t = mx_kscale(G0), mx_kscale(HID)
    return {"x0": bf(np.random.standard_normal((B, G0)) * s),
            "w1_g0": bf(np.random.standard_normal((HID, G0)) / np.sqrt(G0) / s),
            "w3_g0": bf(np.random.standard_normal((HID, G0)) / np.sqrt(G0) / s * t[:, None]),
            "w2_g0": bf(np.random.standard_normal((D, HID)) * W2S / np.sqrt(HID) / t),
            "norm_w": bf(1.0 + 0.1 * np.random.standard_normal(D)),
            "norm_b": bf(0.1 * np.random.standard_normal(D)),
            "term_embed0": bf(np.random.standard_normal(D))}


def reference(x0, w1_g0, w3_g0, w2_g0, norm_w, norm_b, term_embed0):
    xq = mxq(f64(x0), 1, "e4m3")
    gate0 = silu(xq @ mxq(f64(w1_g0), 1, "e4m3").T)
    h = gate0 * (xq @ mxq(f64(w3_g0), 1, "e4m3").T)
    tok = mxq(h, 1, "e4m3") @ mxq(f64(w2_g0), 1, "e4m3").T
    rms = np.sqrt(np.mean(tok * tok, axis=-1, keepdims=True) + EPS)
    return (tok / rms) * f64(norm_w) + f64(norm_b) + f64(term_embed0)

@@ -1,0 +1,250 @@
+from contextlib import ExitStack
+
+import concourse.mybir as mybir
+from concourse.masks import make_identity
+
+B, G0, HID, D = 256, 512, 2048, 1024
+EPS = 1e-05
+FLOPS = 2 * B * G0 * HID * 2 + 2 * B * HID * D
+
+F32 = mybir.dt.float32
+BF16 = mybir.dt.bfloat16
+U32 = mybir.dt.uint32
+U8 = mybir.dt.uint8
+FP8X4 = mybir.dt.float8_e4m3fn_x4
+ACT = mybir.ActivationFunctionType
+ALU = mybir.AluOpType
+
+P = 128
+NB = 512
+STAGE1_BANK = F32
+SORTED_RUNS = ((0, 1), (1, 0), (1, 1))
+EVAC = {"p4": "SSSS", "p5": "SSSS", "p6": "SSSS", "p7": "SVSS"}
+FILL = {"p4": (0, 1), "p5": (1, 0), "p6": (1, 1)}
+
+
+def tile_observationembeddingv2_pa_kernel(tc, x0, w1_g0, w3_g0, w2_g0, norm_w, norm_b, term_embed0, out):
+    nc = tc.nc
+    with ExitStack() as ctx:
+        keep = ctx.enter_context(tc.tile_pool(name="keep", bufs=1))
+        rot = ctx.enter_context(tc.tile_pool(name="rot", bufs=4))
+        psum = ctx.enter_context(tc.psum_pool(name="psum", bufs=8))
+
+        def bank_tile(dtype, name):
+            return psum.tile([P, NB], dtype, tag="bank", name=name)
+
+        x_raw = keep.tile([P, 2, G0], BF16, name="x_raw")
+        w1_raw = [keep.tile([P, 4, G0], BF16, name="w1_raw%d" % c) for c in range(4)]
+        w3_raw = [keep.tile([P, 4, G0], BF16, name="w3_raw%d" % c) for c in range(4)]
+        w2_raw = [keep.tile([P, HID], BF16, name="w2_raw%d" % r) for r in range(8)]
+        w2_sorted = [keep.tile([P, HID], BF16, name="w2_sorted%d" % r) for r in range(8)]
+        gain = keep.tile([P, D], BF16, name="gain")
+        shift_rows = keep.tile([P, D], BF16, name="shift_rows")
+        ones = keep.tile([P, P], BF16, name="ones")
+        ident = keep.tile([P, P], F32, name="ident")
+        unit = keep.tile([P, 1], F32, name="unit")
+        warm = keep.tile([P, 2], F32, name="warm")
+
+        def mx_tiles(width, name):
+            codes = keep.tile([P, width], U32, name=name + "_c", align_bytes=64)
+            scales = keep.tile([P, width], U8, name=name + "_s", align_bytes=64)
+            return codes, scales
+
+        x_q = mx_tiles(B, "x_q")
+        w1_q = [mx_tiles(NB, "w1_q%d" % c) for c in range(4)]
+        w3_q = [mx_tiles(NB, "w3_q%d" % c) for c in range(4)]
+        h_q = [mx_tiles(B, "h_q%d" % c) for c in range(4)]
+        w2_q = dict(((dc, g), mx_tiles(NB, "w2_q%d_%d" % (dc, g))) for dc in range(2) for g in range(4))
+        h_sb = [keep.tile([P, 2, NB], BF16, name="h_sb%d" % c) for c in range(4)]
+        tokw = dict(((bt, dc), keep.tile([P, NB], F32, name="tokw%d_%d" % (bt, dc))) for bt in range(2) for dc in range(2))
+        msq = dict(((bt, dc), keep.tile([P, 1], F32, name="msq%d_%d" % (bt, dc))) for bt in range(2) for dc in range(2))
+        msq_eps = [keep.tile([P, 1], F32, name="msq_eps%d" % bt) for bt in range(2)]
+        rms = [keep.tile([P, 1], F32, name="rms%d" % bt) for bt in range(2)]
+        rstd = [keep.tile([P, 1], F32, name="rstd%d" % bt) for bt in range(2)]
+
+        out_v = out.rearrange("(q t) d -> q t d", t=2)
+
+        make_identity(nc, ident[:])
+        nc.vector.memset(unit[:], 1.0)
+        nc.vector.memset(ones[:], 1.0)
+        nc.vector.memset(shift_rows[:], 0.0)
+
+        ctx.enter_context(tc.manual_schedule())
+
+        nc.sync.dma_start(out=x_raw[:], in_=x0.rearrange("(q t) k -> q t k", t=2))
+        for c in range(4):
+            rows = slice(c * NB, (c + 1) * NB)
+            nc.sync.dma_start(out=w1_raw[c][:], in_=w1_g0[rows, :].rearrange("(q r) k -> q r k", r=4))
+            nc.sync.dma_start(out=w3_raw[c][:], in_=w3_g0[rows, :].rearrange("(q r) k -> q r k", r=4))
+        for r in range(8):
+            nc.sync.dma_start(out=w2_raw[r][:], in_=w2_g0[r * P:(r + 1) * P, :])
+        nc.sync.dma_start(out=gain[:], in_=norm_w.partition_broadcast(P))
+        nc.sync.dma_start(out=shift_rows[0:1, :], in_=norm_b.rearrange("(o d) -> o d", o=1))
+        nc.sync.dma_start(out=shift_rows[1:2, :], in_=term_embed0.rearrange("(o d) -> o d", o=1))
+
+        nc.scalar.activation(out=warm[:, 0:1], in_=unit[:], func=ACT.Silu)
+
+        def transpose_bank(srcs, name):
+            bank = bank_tile(F32, name)
+            view = bank[:].rearrange("p (a w q) -> p a w q", a=2, w=2)
+            for a in range(2):
+                for w in range(2):
+                    nc.tensor.transpose(view[:, a, w, :], srcs(a, w), ident[:])
+            return bank
+
+        def evacuate(engine, bank, grouped, half, woven):
+            copy = nc.scalar.copy if engine == "S" else nc.vector.tensor_copy
+            dst = grouped[:].bitcast(F32)[:, half * NB:(half + 1) * NB]
+            if woven:
+                copy(out=dst.rearrange("p (q a w) -> p q a w", a=2, w=2),
+                     in_=bank[:].rearrange("p (a w q) -> p q a w", a=2, w=2))
+            else:
+                copy(out=dst.rearrange("p (a q w) -> p a q w", a=2, w=2),
+                     in_=bank[:].rearrange("p (a w q) -> p a q w", a=2, w=2))
+
+        def quantize(grouped, target):
+            nc.vector.quantize_mx(out=target[0][:].bitcast(FP8X4), scales=target[1][:], in_=grouped[:])
+
+        def every_2nd_word(rows_ap, first, w):
+            return rows_ap.bitcast(F32)[:, first + w:first + 256:2]
+
+        def w13_group(raw, target):
+            return (lambda half: (lambda a, w: every_2nd_word(raw[:, 2 * half + a, :], 0, w)), True, target)
+
+        def sort_words(r, pair):
+            cols = slice(pair * NB, (pair + 1) * NB)
+            nc.vector.tensor_copy(out=w2_sorted[r][:].bitcast(F32)[:, cols].rearrange("p (g w q) -> p g w q", g=2, w=2),
+                                  in_=w2_raw[r][:].bitcast(F32)[:, cols].rearrange("p (g q w) -> p g w q", g=2, w=2))
+
+        def w2_group(dc, g):
+            if (dc, g // 2) in SORTED_RUNS:
+                return (lambda half: (lambda a, w: w2_sorted[4 * dc + 2 * half + a][:].bitcast(F32)[
+                    :, 256 * g + P * w:256 * g + P * (w + 1)]), False, w2_q[(dc, g)])
+            return (lambda half: (lambda a, w: every_2nd_word(w2_raw[4 * dc + 2 * half + a][:], 256 * g, w)),
+                    False, w2_q[(dc, g)])
+
+        def grouped_tile(width, name):
+            return rot.tile([P, width], BF16, tag="grp", name=name, bufs=6, align_bytes=64)
+
+        def small_operand(srcs, target, name):
+            bank = transpose_bank(srcs, name + "_t")
+            grouped = grouped_tile(4 * B, name + "_g")
+            evacuate("S", bank, grouped, 0, False)
+            quantize(grouped, target)
+
+        def stage1_matmuls(c):
+            banks = []
+            for nm, wq in (("gate", w1_q[c]), ("up", w3_q[c])):
+                for bt in range(2):
+                    bank = bank_tile(STAGE1_BANK, "%s%d_%d" % (nm, c, bt))
+                    cols = slice(bt * P, (bt + 1) * P)
+                    nc.tensor.matmul_mx(out=bank[:], lhsT=x_q[0][:, cols].bitcast(FP8X4), lhsT_scale=x_q[1][:, cols],
+                                        rhs=wq[0][:].bitcast(FP8X4), rhs_scale=wq[1][:], start=True, stop=True)
+                    banks.append(bank)
+            return banks
+
+        def gated(c, bt, banks):
+            act = rot.tile([P, NB], F32, tag="act", name="act%d_%d" % (c, bt))
+            nc.scalar.activation(out=act[:], in_=banks[bt][:], func=ACT.Silu)
+            nc.vector.tensor_tensor(out=h_sb[c][:, bt, :], in0=banks[2 + bt][:], in1=act[:], op=ALU.mult)
+
+        acc = {}
+
+        def stage2_matmul(bt, dc, g):
+            if g == 0:
+                acc[(bt, dc)] = bank_tile(F32, "tok%d_%d" % (bt, dc))
+            cols = slice(bt * P, (bt + 1) * P)
+            nc.tensor.matmul_mx(out=acc[(bt, dc)][:], lhsT=h_q[g][0][:, cols].bitcast(FP8X4),
+                                lhsT_scale=h_q[g][1][:, cols], rhs=w2_q[(dc, g)][0][:].bitcast(FP8X4),
+                                rhs_scale=w2_q[(dc, g)][1][:], start=(g == 0), stop=(g == 3))
+
+        def mean_square(bt, dc):
+            junk = rot.tile([P, NB], BF16, tag="junk", name="junk%d_%d" % (bt, dc), bufs=2)
+            nc.scalar.activation(out=junk[:], in_=acc[(bt, dc)][:], func=ACT.Square, scale=1.0 / 32.0,
+                                 accum_out=msq[(bt, dc)][:])
+
+        def times_gain(bt, dc):
+            nc.vector.tensor_tensor(out=tokw[(bt, dc)][:], in0=acc[(bt, dc)][:], in1=gain[:, dc * NB:(dc + 1) * NB],
+                                    op=ALU.mult)
+
+        def period(groups, name, chunk_m=None, stage2=(), chunk_t=None, after_gate=None):
+            engines = EVAC.get(name, "SSSV")
+            fill = []
+            if name in FILL:
+                dc_f, pair_f = FILL[name]
+                fill = [(4 * dc_f + i, pair_f) for i in range(4)]
+            banks = []
+            for i in range(2):
+                for half in range(2):
+                    banks.append(transpose_bank(groups[i][0](half), "%s_t%d%d" % (name, i, half)))
+            grp_a = grouped_tile(4 * NB, name + "_ga")
+            grp_b = grouped_tile(4 * NB, name + "_gb")
+            for r, pair in fill[0:2]:
+                sort_words(r, pair)
+            evacuate(engines[0], banks[0], grp_a, 0, groups[0][1])
+            evacuate(engines[1], banks[1], grp_a, 1, groups[0][1])
+            quantize(grp_a, groups[0][2])
+            evacuate(engines[2], banks[2], grp_b, 0, groups[1][1])
+            evacuate(engines[3], banks[3], grp_b, 1, groups[1][1])
+            for r, pair in fill[2:4]:
+                sort_words(r, pair)
+            if chunk_m is not None:
+                s1 = stage1_matmuls(chunk_m)
+                gated(chunk_m, 0, s1)
+                quantize(grp_b, groups[1][2])
+                gated(chunk_m, 1, s1)
+            else:
+                for bt, dc, g in stage2:
+                    stage2_matmul(bt, dc, g)
+                quantize(grp_b, groups[1][2])
+            if after_gate is not None:
+                after_gate()
+            if chunk_t is not None:
+                c = chunk_t
+                small_operand(lambda bt, u: h_sb[c][:, bt, :].bitcast(F32)[:, u * P:(u + 1) * P], h_q[c], "h%d" % c)
+
+
+        small_operand(lambda t, w: every_2nd_word(x_raw[:, t, :], 0, w), x_q, "x")
+        s1_groups = [(w13_group(w1_raw[c], w1_q[c]), w13_group(w3_raw[c], w3_q[c])) for c in range(4)]
+        period(s1_groups[0], "p0")
+        period(s1_groups[1], "p1", chunk_m=0)
+        period(s1_groups[2], "p2", chunk_m=1, chunk_t=0)
+        period(s1_groups[3], "p3", chunk_m=2, chunk_t=1)
+        period((w2_group(0, 0), w2_group(0, 1)), "p4", chunk_m=3, chunk_t=2)
+        period((w2_group(0, 2), w2_group(0, 3)), "p5", stage2=((0, 0, 0), (0, 0, 1), (1, 0, 0), (1, 0, 1)), chunk_t=3)
+        period((w2_group(1, 0), w2_group(1, 1)), "p6", stage2=((0, 0, 2), (0, 0, 3), (1, 0, 2), (1, 0, 3)))
+        for bt in range(2):
+            mean_square(bt, 0)
+            nc.gpsimd.tensor_scalar_add(out=msq_eps[bt][:], in0=msq[(bt, 0)][:], scalar1=EPS)
+        period((w2_group(1, 2), w2_group(1, 3)), "p7")
+        nc.scalar.activation(out=warm[:, 1:2], in_=unit[:], func=ACT.Sqrt)
+        times_gain(0, 0)
+        times_gain(1, 0)
+        for bt, g in ((0, 0), (0, 1), (1, 0), (1, 1), (0, 2), (1, 2), (0, 3), (1, 3)):
+            stage2_matmul(bt, 1, g)
+        shift = []
+        for dc in range(2):
+            shift.append(bank_tile(F32, "shift%d" % dc))
+            nc.tensor.matmul(out=shift[dc][:], lhsT=ones[:], rhs=shift_rows[:, dc * NB:(dc + 1) * NB], start=True, stop=True)
+
+        def finish(bt, dc):
+            res = rot.tile([P, NB], F32, tag="res", name="res%d_%d" % (bt, dc))
+            nc.vector.scalar_tensor_tensor(out=res[:], in0=tokw[(bt, dc)][:], scalar=rstd[bt][:], in1=shift[dc][:],
+                                           op0=ALU.mult, op1=ALU.add)
+            nc.sync.dma_start(out=out_v[:, bt, dc * NB:(dc + 1) * NB], in_=res[:])
+
+        def root(bt):
+            nc.scalar.activation(out=rms[bt][:], in_=msq[(bt, 1)][:], func=ACT.Sqrt, bias=msq_eps[bt][:], scale=1.0)
+
+        mean_square(0, 1)
+        root(0)
+        times_gain(1, 1)
+        mean_square(1, 1)
+        root(1)
+        nc.vector.reciprocal(out=rstd[0][:], in_=rms[0][:])
+        finish(0, 0)
+        times_gain(0, 1)
+        finish(0, 1)
+        nc.vector.reciprocal(out=rstd[1][:], in_=rms[1][:])
+        finish(1, 0)
+        finish(1, 1)

@@ -18,9 +18,6 @@ ALU = mybir.AluOpType
 P = 128
 NB = 512
 STAGE1_BANK = F32
-SORTED_RUNS = ((0, 1), (1, 0), (1, 1))
-EVAC = {"p4": "SSSS", "p5": "SSSS", "p6": "SSSS", "p7": "SVSS"}
-FILL = {"p4": (0, 1), "p5": (1, 0), "p6": (1, 1)}
 
 
 def tile_observationembeddingv2_pa_kernel(tc, x0, w1_g0, w3_g0, w2_g0, norm_w, norm_b, term_embed0, out):
@@ -37,6 +34,7 @@ def tile_observationembeddingv2_pa_kernel(tc, x0, w1_g0, w3_g0, w2_g0, norm_w, n
         w1_raw = [keep.tile([P, 4, G0], BF16, name="w1_raw%d" % c) for c in range(4)]
         w3_raw = [keep.tile([P, 4, G0], BF16, name="w3_raw%d" % c) for c in range(4)]
         w2_raw = [keep.tile([P, HID], BF16, name="w2_raw%d" % r) for r in range(8)]
+        w3_sorted = dict((c, keep.tile([P, HID], BF16, name="w3_sorted%d" % c)) for c in (2, 3))
         w2_sorted = [keep.tile([P, HID], BF16, name="w2_sorted%d" % r) for r in range(8)]
         gain = keep.tile([P, D], BF16, name="gain")
         shift_rows = keep.tile([P, D], BF16, name="shift_rows")
@@ -108,18 +106,30 @@ def tile_observationembeddingv2_pa_kernel(tc, x0, w1_g0, w3_g0, w2_g0, norm_w, n
         def every_2nd_word(rows_ap, first, w):
             return rows_ap.bitcast(F32)[:, first + w:first + 256:2]
 
-        def w13_group(raw, target):
+        def sorted_words(tile_ap, block, w):
+            return tile_ap.bitcast(F32)[:, 256 * block + P * w:256 * block + P * (w + 1)]
+
+        def sort_words(dst, src, part):
+            cols = slice(part * NB, (part + 1) * NB)
+            nc.vector.tensor_copy(out=dst.bitcast(F32)[:, cols].rearrange("p (g w q) -> p g w q", g=2, w=2),
+                                  in_=src.bitcast(F32)[:, cols].rearrange("p (g q w) -> p g w q", g=2, w=2))
+
+        def sort_w3(c):
+            return [lambda part=part: sort_words(w3_sorted[c][:], w3_raw[c][:].rearrange("p r k -> p (r k)"), part)
+                    for part in range(2)]
+
+        def sort_w2(dc, pair):
+            return [lambda r=r: sort_words(w2_sorted[r][:], w2_raw[r][:], pair) for r in range(4 * dc, 4 * dc + 4)]
+
+        def w13_group(raw, target, in_order=None):
+            if in_order is not None:
+                return (lambda half: (lambda a, w: sorted_words(in_order[:], 2 * half + a, w)), True, target)
             return (lambda half: (lambda a, w: every_2nd_word(raw[:, 2 * half + a, :], 0, w)), True, target)
 
-        def sort_words(r, pair):
-            cols = slice(pair * NB, (pair + 1) * NB)
-            nc.vector.tensor_copy(out=w2_sorted[r][:].bitcast(F32)[:, cols].rearrange("p (g w q) -> p g w q", g=2, w=2),
-                                  in_=w2_raw[r][:].bitcast(F32)[:, cols].rearrange("p (g q w) -> p g w q", g=2, w=2))
-
-        def w2_group(dc, g):
-            if (dc, g // 2) in SORTED_RUNS:
-                return (lambda half: (lambda a, w: w2_sorted[4 * dc + 2 * half + a][:].bitcast(F32)[
-                    :, 256 * g + P * w:256 * g + P * (w + 1)]), False, w2_q[(dc, g)])
+        def w2_group(dc, g, in_order):
+            if in_order:
+                return (lambda half: (lambda a, w: sorted_words(w2_sorted[4 * dc + 2 * half + a][:], g, w)),
+                        False, w2_q[(dc, g)])
             return (lambda half: (lambda a, w: every_2nd_word(w2_raw[4 * dc + 2 * half + a][:], 256 * g, w)),
                     False, w2_q[(dc, g)])
 
@@ -167,27 +177,22 @@ def tile_observationembeddingv2_pa_kernel(tc, x0, w1_g0, w3_g0, w2_g0, norm_w, n
             nc.vector.tensor_tensor(out=tokw[(bt, dc)][:], in0=acc[(bt, dc)][:], in1=gain[:, dc * NB:(dc + 1) * NB],
                                     op=ALU.mult)
 
-        def period(groups, name, chunk_m=None, stage2=(), chunk_t=None, after_gate=None):
-            engines = EVAC.get(name, "SSSV")
-            fill = []
-            if name in FILL:
-                dc_f, pair_f = FILL[name]
-                fill = [(4 * dc_f + i, pair_f) for i in range(4)]
+        def period(groups, name, engines, chunk_m=None, stage2=(), chunk_t=None, sorts_early=(), sorts_late=()):
             banks = []
             for i in range(2):
                 for half in range(2):
                     banks.append(transpose_bank(groups[i][0](half), "%s_t%d%d" % (name, i, half)))
             grp_a = grouped_tile(4 * NB, name + "_ga")
             grp_b = grouped_tile(4 * NB, name + "_gb")
-            for r, pair in fill[0:2]:
-                sort_words(r, pair)
+            for sort in sorts_early:
+                sort()
             evacuate(engines[0], banks[0], grp_a, 0, groups[0][1])
             evacuate(engines[1], banks[1], grp_a, 1, groups[0][1])
             quantize(grp_a, groups[0][2])
             evacuate(engines[2], banks[2], grp_b, 0, groups[1][1])
             evacuate(engines[3], banks[3], grp_b, 1, groups[1][1])
-            for r, pair in fill[2:4]:
-                sort_words(r, pair)
+            for sort in sorts_late:
+                sort()
             if chunk_m is not None:
                 s1 = stage1_matmuls(chunk_m)
                 gated(chunk_m, 0, s1)
@@ -197,26 +202,28 @@ def tile_observationembeddingv2_pa_kernel(tc, x0, w1_g0, w3_g0, w2_g0, norm_w, n
                 for bt, dc, g in stage2:
                     stage2_matmul(bt, dc, g)
                 quantize(grp_b, groups[1][2])
-            if after_gate is not None:
-                after_gate()
             if chunk_t is not None:
                 c = chunk_t
                 small_operand(lambda bt, u: h_sb[c][:, bt, :].bitcast(F32)[:, u * P:(u + 1) * P], h_q[c], "h%d" % c)
 
-
         small_operand(lambda t, w: every_2nd_word(x_raw[:, t, :], 0, w), x_q, "x")
-        s1_groups = [(w13_group(w1_raw[c], w1_q[c]), w13_group(w3_raw[c], w3_q[c])) for c in range(4)]
-        period(s1_groups[0], "p0")
-        period(s1_groups[1], "p1", chunk_m=0)
-        period(s1_groups[2], "p2", chunk_m=1, chunk_t=0)
-        period(s1_groups[3], "p3", chunk_m=2, chunk_t=1)
-        period((w2_group(0, 0), w2_group(0, 1)), "p4", chunk_m=3, chunk_t=2)
-        period((w2_group(0, 2), w2_group(0, 3)), "p5", stage2=((0, 0, 0), (0, 0, 1), (1, 0, 0), (1, 0, 1)), chunk_t=3)
-        period((w2_group(1, 0), w2_group(1, 1)), "p6", stage2=((0, 0, 2), (0, 0, 3), (1, 0, 2), (1, 0, 3)))
+        s1_groups = [(w13_group(w1_raw[c], w1_q[c]), w13_group(w3_raw[c], w3_q[c], w3_sorted.get(c))) for c in range(4)]
+        period(s1_groups[0], "p0", "SSSV")
+        period(s1_groups[1], "p1", "SSSV", chunk_m=0, sorts_late=sort_w3(2))
+        period(s1_groups[2], "p2", "SSSV", chunk_m=1, chunk_t=0, sorts_late=sort_w3(3))
+        period(s1_groups[3], "p3", "SSSV", chunk_m=2, chunk_t=1)
+        period((w2_group(0, 0, False), w2_group(0, 1, False)), "p4", "SSSS", chunk_m=3, chunk_t=2,
+               sorts_early=sort_w2(0, 1)[0:2], sorts_late=sort_w2(0, 1)[2:4])
+        period((w2_group(0, 2, True), w2_group(0, 3, True)), "p5", "SSSS",
+               stage2=((0, 0, 0), (0, 0, 1), (1, 0, 0), (1, 0, 1)), chunk_t=3,
+               sorts_early=sort_w2(1, 0)[0:2], sorts_late=sort_w2(1, 0)[2:4])
+        period((w2_group(1, 0, True), w2_group(1, 1, True)), "p6", "SSSS",
+               stage2=((0, 0, 2), (0, 0, 3), (1, 0, 2), (1, 0, 3)),
+               sorts_early=sort_w2(1, 1)[0:2], sorts_late=sort_w2(1, 1)[2:4])
         for bt in range(2):
             mean_square(bt, 0)
             nc.gpsimd.tensor_scalar_add(out=msq_eps[bt][:], in0=msq[(bt, 0)][:], scalar1=EPS)
-        period((w2_group(1, 2), w2_group(1, 3)), "p7")
+        period((w2_group(1, 2, True), w2_group(1, 3, True)), "p7", "SVSS")
         nc.scalar.activation(out=warm[:, 1:2], in_=unit[:], func=ACT.Sqrt)
         times_gain(0, 0)
         times_gain(1, 0)

from contextlib import ExitStack

import concourse.mybir as mybir
from concourse.masks import make_identity

B, G0, HID, D = 256, 512, 2048, 1024
EPS = 1e-05
FLOPS = 2 * B * G0 * HID * 2 + 2 * B * HID * D

F32 = mybir.dt.float32
BF16 = mybir.dt.bfloat16
U32 = mybir.dt.uint32
U8 = mybir.dt.uint8
FP8X4 = mybir.dt.float8_e4m3fn_x4
ACT = mybir.ActivationFunctionType
ALU = mybir.AluOpType

P = 128
NB = 512
STAGE1_BANK = F32


def tile_observationembeddingv2_pa_kernel(tc, x0, w1_g0, w3_g0, w2_g0, norm_w, norm_b, term_embed0, out):
    nc = tc.nc
    with ExitStack() as ctx:
        keep = ctx.enter_context(tc.tile_pool(name="keep", bufs=1))
        rot = ctx.enter_context(tc.tile_pool(name="rot", bufs=4))
        psum = ctx.enter_context(tc.psum_pool(name="psum", bufs=8))

        def bank_tile(dtype, name):
            return psum.tile([P, NB], dtype, tag="bank", name=name)

        x_raw = keep.tile([P, 2, G0], BF16, name="x_raw")
        w1_raw = [keep.tile([P, 4, G0], BF16, name="w1_raw%d" % c) for c in range(4)]
        w3_raw = [keep.tile([P, 4, G0], BF16, name="w3_raw%d" % c) for c in range(4)]
        w2_raw = [keep.tile([P, HID], BF16, name="w2_raw%d" % r) for r in range(8)]
        w3_sorted = dict((c, keep.tile([P, HID], BF16, name="w3_sorted%d" % c)) for c in (2, 3))
        w2_sorted = [keep.tile([P, HID], BF16, name="w2_sorted%d" % r) for r in range(8)]
        gain = keep.tile([P, D], BF16, name="gain")
        shift_rows = keep.tile([P, D], BF16, name="shift_rows")
        ones = keep.tile([P, P], BF16, name="ones")
        ident = keep.tile([P, P], F32, name="ident")
        unit = keep.tile([P, 1], F32, name="unit")
        warm = keep.tile([P, 2], F32, name="warm")

        def mx_tiles(width, name):
            codes = keep.tile([P, width], U32, name=name + "_c", align_bytes=64)
            scales = keep.tile([P, width], U8, name=name + "_s", align_bytes=64)
            return codes, scales

        x_q = mx_tiles(B, "x_q")
        w1_q = [mx_tiles(NB, "w1_q%d" % c) for c in range(4)]
        w3_q = [mx_tiles(NB, "w3_q%d" % c) for c in range(4)]
        h_q = [mx_tiles(B, "h_q%d" % c) for c in range(4)]
        w2_q = dict(((dc, g), mx_tiles(NB, "w2_q%d_%d" % (dc, g))) for dc in range(2) for g in range(4))
        h_sb = [keep.tile([P, 2, NB], BF16, name="h_sb%d" % c) for c in range(4)]
        tokw = dict(((bt, dc), keep.tile([P, NB], F32, name="tokw%d_%d" % (bt, dc))) for bt in range(2) for dc in range(2))
        msq = dict(((bt, dc), keep.tile([P, 1], F32, name="msq%d_%d" % (bt, dc))) for bt in range(2) for dc in range(2))
        msq_eps = [keep.tile([P, 1], F32, name="msq_eps%d" % bt) for bt in range(2)]
        rms = [keep.tile([P, 1], F32, name="rms%d" % bt) for bt in range(2)]
        rstd = [keep.tile([P, 1], F32, name="rstd%d" % bt) for bt in range(2)]

        out_v = out.rearrange("(q t) d -> q t d", t=2)

        make_identity(nc, ident[:])
        nc.vector.memset(unit[:], 1.0)
        nc.vector.memset(ones[:], 1.0)
        nc.vector.memset(shift_rows[:], 0.0)

        ctx.enter_context(tc.manual_schedule())

        nc.sync.dma_start(out=x_raw[:], in_=x0.rearrange("(q t) k -> q t k", t=2))
        for c in range(4):
            rows = slice(c * NB, (c + 1) * NB)
            nc.sync.dma_start(out=w1_raw[c][:], in_=w1_g0[rows, :].rearrange("(q r) k -> q r k", r=4))
            nc.sync.dma_start(out=w3_raw[c][:], in_=w3_g0[rows, :].rearrange("(q r) k -> q r k", r=4))
        for r in range(8):
            nc.sync.dma_start(out=w2_raw[r][:], in_=w2_g0[r * P:(r + 1) * P, :])
        nc.sync.dma_start(out=gain[:], in_=norm_w.partition_broadcast(P))
        nc.sync.dma_start(out=shift_rows[0:1, :], in_=norm_b.rearrange("(o d) -> o d", o=1))
        nc.sync.dma_start(out=shift_rows[1:2, :], in_=term_embed0.rearrange("(o d) -> o d", o=1))

        nc.scalar.activation(out=warm[:, 0:1], in_=unit[:], func=ACT.Silu)

        def transpose_bank(srcs, name):
            bank = bank_tile(F32, name)
            view = bank[:].rearrange("p (a w q) -> p a w q", a=2, w=2)
            for a in range(2):
                for w in range(2):
                    nc.tensor.transpose(view[:, a, w, :], srcs(a, w), ident[:])
            return bank

        def evacuate(engine, bank, grouped, half, woven):
            copy = nc.scalar.copy if engine == "S" else nc.vector.tensor_copy
            dst = grouped[:].bitcast(F32)[:, half * NB:(half + 1) * NB]
            if woven:
                copy(out=dst.rearrange("p (q a w) -> p q a w", a=2, w=2),
                     in_=bank[:].rearrange("p (a w q) -> p q a w", a=2, w=2))
            else:
                copy(out=dst.rearrange("p (a q w) -> p a q w", a=2, w=2),
                     in_=bank[:].rearrange("p (a w q) -> p a q w", a=2, w=2))

        def quantize(grouped, target):
            nc.vector.quantize_mx(out=target[0][:].bitcast(FP8X4), scales=target[1][:], in_=grouped[:])

        def every_2nd_word(rows_ap, first, w):
            return rows_ap.bitcast(F32)[:, first + w:first + 256:2]

        def sorted_words(tile_ap, block, w):
            return tile_ap.bitcast(F32)[:, 256 * block + P * w:256 * block + P * (w + 1)]

        def sort_words(dst, src, part):
            cols = slice(part * NB, (part + 1) * NB)
            nc.vector.tensor_copy(out=dst.bitcast(F32)[:, cols].rearrange("p (g w q) -> p g w q", g=2, w=2),
                                  in_=src.bitcast(F32)[:, cols].rearrange("p (g q w) -> p g w q", g=2, w=2))

        def sort_w3(c):
            return [lambda part=part: sort_words(w3_sorted[c][:], w3_raw[c][:].rearrange("p r k -> p (r k)"), part)
                    for part in range(2)]

        def sort_w2(dc, pair):
            return [lambda r=r: sort_words(w2_sorted[r][:], w2_raw[r][:], pair) for r in range(4 * dc, 4 * dc + 4)]

        def w13_group(raw, target, in_order=None):
            if in_order is not None:
                return (lambda half: (lambda a, w: sorted_words(in_order[:], 2 * half + a, w)), True, target)
            return (lambda half: (lambda a, w: every_2nd_word(raw[:, 2 * half + a, :], 0, w)), True, target)

        def w2_group(dc, g, in_order):
            if in_order:
                return (lambda half: (lambda a, w: sorted_words(w2_sorted[4 * dc + 2 * half + a][:], g, w)),
                        False, w2_q[(dc, g)])
            return (lambda half: (lambda a, w: every_2nd_word(w2_raw[4 * dc + 2 * half + a][:], 256 * g, w)),
                    False, w2_q[(dc, g)])

        def grouped_tile(width, name):
            return rot.tile([P, width], BF16, tag="grp", name=name, bufs=6, align_bytes=64)

        def small_operand(srcs, target, name):
            bank = transpose_bank(srcs, name + "_t")
            grouped = grouped_tile(4 * B, name + "_g")
            evacuate("S", bank, grouped, 0, False)
            quantize(grouped, target)

        def stage1_matmuls(c):
            banks = []
            for nm, wq in (("gate", w1_q[c]), ("up", w3_q[c])):
                for bt in range(2):
                    bank = bank_tile(STAGE1_BANK, "%s%d_%d" % (nm, c, bt))
                    cols = slice(bt * P, (bt + 1) * P)
                    nc.tensor.matmul_mx(out=bank[:], lhsT=x_q[0][:, cols].bitcast(FP8X4), lhsT_scale=x_q[1][:, cols],
                                        rhs=wq[0][:].bitcast(FP8X4), rhs_scale=wq[1][:], start=True, stop=True)
                    banks.append(bank)
            return banks

        def gated(c, bt, banks):
            act = rot.tile([P, NB], F32, tag="act", name="act%d_%d" % (c, bt))
            nc.scalar.activation(out=act[:], in_=banks[bt][:], func=ACT.Silu)
            nc.vector.tensor_tensor(out=h_sb[c][:, bt, :], in0=banks[2 + bt][:], in1=act[:], op=ALU.mult)

        acc = {}

        def stage2_matmul(bt, dc, g):
            if g == 0:
                acc[(bt, dc)] = bank_tile(F32, "tok%d_%d" % (bt, dc))
            cols = slice(bt * P, (bt + 1) * P)
            nc.tensor.matmul_mx(out=acc[(bt, dc)][:], lhsT=h_q[g][0][:, cols].bitcast(FP8X4),
                                lhsT_scale=h_q[g][1][:, cols], rhs=w2_q[(dc, g)][0][:].bitcast(FP8X4),
                                rhs_scale=w2_q[(dc, g)][1][:], start=(g == 0), stop=(g == 3))

        def mean_square(bt, dc):
            junk = rot.tile([P, NB], BF16, tag="junk", name="junk%d_%d" % (bt, dc), bufs=2)
            nc.scalar.activation(out=junk[:], in_=acc[(bt, dc)][:], func=ACT.Square, scale=1.0 / 32.0,
                                 accum_out=msq[(bt, dc)][:])

        def times_gain(bt, dc):
            nc.vector.tensor_tensor(out=tokw[(bt, dc)][:], in0=acc[(bt, dc)][:], in1=gain[:, dc * NB:(dc + 1) * NB],
                                    op=ALU.mult)

        def period(groups, name, engines, chunk_m=None, stage2=(), chunk_t=None, sorts_early=(), sorts_late=()):
            banks = []
            for i in range(2):
                for half in range(2):
                    banks.append(transpose_bank(groups[i][0](half), "%s_t%d%d" % (name, i, half)))
            grp_a = grouped_tile(4 * NB, name + "_ga")
            grp_b = grouped_tile(4 * NB, name + "_gb")
            for sort in sorts_early:
                sort()
            evacuate(engines[0], banks[0], grp_a, 0, groups[0][1])
            evacuate(engines[1], banks[1], grp_a, 1, groups[0][1])
            quantize(grp_a, groups[0][2])
            evacuate(engines[2], banks[2], grp_b, 0, groups[1][1])
            evacuate(engines[3], banks[3], grp_b, 1, groups[1][1])
            for sort in sorts_late:
                sort()
            if chunk_m is not None:
                s1 = stage1_matmuls(chunk_m)
                gated(chunk_m, 0, s1)
                quantize(grp_b, groups[1][2])
                gated(chunk_m, 1, s1)
            else:
                for bt, dc, g in stage2:
                    stage2_matmul(bt, dc, g)
                quantize(grp_b, groups[1][2])
            if chunk_t is not None:
                c = chunk_t
                small_operand(lambda bt, u: h_sb[c][:, bt, :].bitcast(F32)[:, u * P:(u + 1) * P], h_q[c], "h%d" % c)

        small_operand(lambda t, w: every_2nd_word(x_raw[:, t, :], 0, w), x_q, "x")
        s1_groups = [(w13_group(w1_raw[c], w1_q[c]), w13_group(w3_raw[c], w3_q[c], w3_sorted.get(c))) for c in range(4)]
        period(s1_groups[0], "p0", "SSSV")
        period(s1_groups[1], "p1", "SSSV", chunk_m=0, sorts_late=sort_w3(2))
        period(s1_groups[2], "p2", "SSSV", chunk_m=1, chunk_t=0, sorts_late=sort_w3(3))
        period(s1_groups[3], "p3", "SSSV", chunk_m=2, chunk_t=1)
        period((w2_group(0, 0, False), w2_group(0, 1, False)), "p4", "SSSS", chunk_m=3, chunk_t=2,
               sorts_early=sort_w2(0, 1)[0:2], sorts_late=sort_w2(0, 1)[2:4])
        period((w2_group(0, 2, True), w2_group(0, 3, True)), "p5", "SSSS",
               stage2=((0, 0, 0), (0, 0, 1), (1, 0, 0), (1, 0, 1)), chunk_t=3,
               sorts_early=sort_w2(1, 0)[0:2], sorts_late=sort_w2(1, 0)[2:4])
        period((w2_group(1, 0, True), w2_group(1, 1, True)), "p6", "SSSS",
               stage2=((0, 0, 2), (0, 0, 3), (1, 0, 2), (1, 0, 3)),
               sorts_early=sort_w2(1, 1)[0:2], sorts_late=sort_w2(1, 1)[2:4])
        for bt in range(2):
            mean_square(bt, 0)
            nc.gpsimd.tensor_scalar_add(out=msq_eps[bt][:], in0=msq[(bt, 0)][:], scalar1=EPS)
        period((w2_group(1, 2, True), w2_group(1, 3, True)), "p7", "SVSS")
        nc.scalar.activation(out=warm[:, 1:2], in_=unit[:], func=ACT.Sqrt)
        times_gain(0, 0)
        times_gain(1, 0)
        for bt, g in ((0, 0), (0, 1), (1, 0), (1, 1), (0, 2), (1, 2), (0, 3), (1, 3)):
            stage2_matmul(bt, 1, g)
        shift = []
        for dc in range(2):
            shift.append(bank_tile(F32, "shift%d" % dc))
            nc.tensor.matmul(out=shift[dc][:], lhsT=ones[:], rhs=shift_rows[:, dc * NB:(dc + 1) * NB], start=True, stop=True)

        def finish(bt, dc):
            res = rot.tile([P, NB], F32, tag="res", name="res%d_%d" % (bt, dc))
            nc.vector.scalar_tensor_tensor(out=res[:], in0=tokw[(bt, dc)][:], scalar=rstd[bt][:], in1=shift[dc][:],
                                           op0=ALU.mult, op1=ALU.add)
            nc.sync.dma_start(out=out_v[:, bt, dc * NB:(dc + 1) * NB], in_=res[:])

        def root(bt):
            nc.scalar.activation(out=rms[bt][:], in_=msq[(bt, 1)][:], func=ACT.Sqrt, bias=msq_eps[bt][:], scale=1.0)

        mean_square(0, 1)
        root(0)
        times_gain(1, 1)
        mean_square(1, 1)
        root(1)
        nc.vector.reciprocal(out=rstd[0][:], in_=rms[0][:])
        finish(0, 0)
        times_gain(0, 1)
        finish(0, 1)
        nc.vector.reciprocal(out=rstd[1][:], in_=rms[1][:])
        finish(1, 0)
        finish(1, 1)
